import numpy as np
import ml_dtypes


def mxq(x, axis, fmt="e4m3"):
    dtype, down = {"e4m3": (ml_dtypes.float8_e4m3fn, 7), "e5m2": (ml_dtypes.float8_e5m2, 14)}[fmt]
    v = np.moveaxis(np.asarray(x, np.float32).astype(ml_dtypes.bfloat16).astype(np.float64), axis, -1)
    blocks = v.reshape(v.shape[:-1] + (-1, 32))
    amax = np.abs(blocks).max(-1, keepdims=True)
    byte = np.maximum(np.where(amax > 0, np.frexp(amax)[1] - 1 + 127, 0) - down, 1)
    scale = np.exp2(byte - 127.0)
    codes = (blocks / scale).astype(np.float32).astype(dtype).astype(np.float64)
    return np.moveaxis((codes * scale).reshape(v.shape), -1, axis)


WIDE = False


def mx_kscale(k):
    if not WIDE:
        return np.ones(k)
    levels = np.array([10, -10, 5, -5, 0])
    if k % 512:
        return np.exp2(np.random.permutation(np.resize(levels, k // 32))).repeat(32)
    a = np.empty((k // 512, 16))
    for p in range(k // 512):
        a[p, :8] = np.random.permutation(np.resize(levels, 8))
        for g in range(8):
            far = levels[np.abs(levels - a[p, g]) >= 10]
            a[p, g + 8] = far[np.random.randint(len(far))]
    return np.exp2(a.ravel()).repeat(32)


BF16 = ml_dtypes.bfloat16


def bf(x):
    return np.asarray(x, np.float32).astype(BF16)


def f64(x):
    return np.asarray(x).astype(np.float64)


E2M1 = np.array([0.0, 0.5, 1.0, 1.5, 2.0, 3.0, 4.0, 6.0, -0.0, -0.5, -1.0, -1.5, -2.0, -3.0, -4.0, -6.0])


def pack_weight(w, fmt):
    k, n = w.shape
    w = f64(bf(w)).reshape(k // 32, 32, n)
    amax = np.abs(w).max(1)
    if fmt == "e4m3":
        byte = np.frexp(amax)[1] - 1 + 127 - 7
    else:
        mant, ex = np.frexp(amax / 6.0)
        byte = np.where(mant > 0.5, ex, ex - 1) + 127
    byte = np.clip(np.where(amax > 0, byte, 1), 1, 254)
    scaled = (w * np.exp2(127.0 - byte)[:, None, :]).reshape(k, n).astype(np.float32)
    by_word = np.ascontiguousarray(scaled.reshape(k // 512, 128, 4, n).transpose(0, 1, 3, 2))
    if fmt == "e4m3":
        words = by_word.astype(ml_dtypes.float8_e4m3fn).view(np.uint8)
    else:
        c = by_word.astype(ml_dtypes.float4_e2m1fn).view(np.uint8) & 0xF
        words = c[..., 0::2] | (c[..., 1::2] << 4)
    return np.ascontiguousarray(words), np.ascontiguousarray(byte.astype(np.uint8).reshape(k // 512, 16, n))


def unpack_weight(words, scales, fmt):
    g, p, n, _ = words.shape
    if fmt == "e4m3":
        vals = np.ascontiguousarray(words).view(ml_dtypes.float8_e4m3fn).astype(np.float64)
    else:
        nib = np.empty((g, p, n, 4), np.uint8)
        nib[..., 0::2] = words & 0xF
        nib[..., 1::2] = words >> 4
        vals = E2M1[nib]
    vals = vals * np.repeat(np.exp2(scales.astype(np.float64) - 127.0), 8, axis=1)[..., None]
    return vals.transpose(0, 1, 3, 2).reshape(g * 512, n)
def pack4(w):
    words, scales = pack_weight(w, "e2m1")
    return words.reshape(words.shape[0], 128, -1), scales


def unpack4(words, scales):
    return unpack_weight(words.reshape(words.shape[0], 128, -1, 2), scales, "e2m1")


B, H, W, C, NH, WS, SHIFT, F = 4, 32, 32, 512, 16, 8, 3, 512
S = WS * WS
HD = C // NH
NWIN = B * (H // WS) * (W // WS)
EPS = 1e-5


def layer_norm(x, w, b):
    m = x.mean(-1, keepdims=True)
    v = ((x - m) ** 2).mean(-1, keepdims=True)
    return (x - m) / np.sqrt(v + EPS) * w + b


def erf(z):
    a = np.clip(z, -6.0, 6.0)
    t2 = 2.0 * a * a
    term = a.copy()
    tot = a.copy()
    for n in range(1, 110):
        term = term * t2 / (2 * n + 1)
        tot = tot + term
    return 2.0 / np.sqrt(np.pi) * np.exp(-a * a) * tot


def gelu(v):
    return 0.5 * v * (1.0 + erf(v / np.sqrt(2.0)))


def draw0():
    s = mx_kscale(C)
    t = mx_kscale(C)
    o_heads = bf(0.25 * np.random.standard_normal((NWIN, NH, S, HD)) * s.reshape(NH, 1, HD))
    x = bf(np.random.standard_normal((B, H * W, C)))
    out_w = 2.0 * np.random.standard_normal((C, C)) / np.sqrt(C) / s[None, :]
    out_w_words, out_w_scales = pack4(out_w.T)
    out_b = bf(0.1 * np.random.standard_normal(C))
    norm2_w = bf((1.0 + 0.1 * np.random.standard_normal(C)) * t)
    norm2_b = bf(0.1 * np.random.standard_normal(C) * t)
    fc1_w = np.random.standard_normal((F, C)) / np.sqrt(C) / t[None, :]
    fc1_w_words, fc1_w_scales = pack4(fc1_w.T)
    fc1_b = bf(0.1 * np.random.standard_normal(F))
    return {"o_heads": o_heads,
            "x": x,
            "out_w_words": out_w_words,
            "out_w_scales": out_w_scales,
            "out_b": out_b,
            "norm2_w": norm2_w,
            "norm2_b": norm2_b,
            "fc1_w_words": fc1_w_words,
            "fc1_w_scales": fc1_w_scales,
            "fc1_b": fc1_b}


def core(o_heads, x, out_w_words, out_w_scales, out_b, norm2_w, norm2_b, fc1_w_words, fc1_w_scales, fc1_b):
    o = f64(o_heads).transpose(0, 2, 1, 3).reshape(-1, S, C)
    o = (mxq(o, 2, "e4m3") @ unpack4(out_w_words, out_w_scales)) + f64(out_b)
    o = o.reshape(B, H // WS, W // WS, WS, WS, C)
    o = o.transpose(0, 1, 3, 2, 4, 5).reshape(B, H, W, C)
    o = np.roll(o, (SHIFT, SHIFT), axis=(1, 2))
    x2 = f64(x) + o.reshape(B, H * W, C)
    h2 = layer_norm(x2, f64(norm2_w), f64(norm2_b))
    g = gelu((mxq(h2, 2, "e4m3") @ unpack4(fc1_w_words, fc1_w_scales)) + f64(fc1_b))
    return x2, g


def e4m3fn_bytes(y):
    return np.clip(np.asarray(y, np.float64), -448.0, 448.0).astype(np.float32).astype(ml_dtypes.float8_e4m3fn).view(np.uint8)


def e4m3fn_values(b):
    return np.asarray(b, np.uint8).view(ml_dtypes.float8_e4m3fn).astype(np.float64)


def setup_inputs():
    d = draw0()
    x0 = np.asarray(d['o_heads']).astype(np.float64)
    s = (np.max(np.abs(x0), axis=(0, 2, 3), keepdims=True) / 448.0).astype(np.float32)
    out = {}
    for k, v in d.items():
        if k == 'o_heads':
            out['o_heads_bytes'] = e4m3fn_bytes(x0 / s.astype(np.float64))
            out['o_heads_scale'] = s
        else:
            out[k] = v
    return out


def reference(o_heads_bytes, o_heads_scale, x, out_w_words, out_w_scales, out_b, norm2_w, norm2_b, fc1_w_words, fc1_w_scales, fc1_b):
    return core(e4m3fn_values(o_heads_bytes) * o_heads_scale.astype(np.float64), x, out_w_words, out_w_scales, out_b, norm2_w, norm2_b, fc1_w_words, fc1_w_scales, fc1_b)

@@ -1,0 +1,393 @@
+from contextlib import ExitStack
+
+import concourse.mybir as mybir
+from concourse.masks import make_identity
+
+F32 = mybir.dt.float32
+BF16 = mybir.dt.bfloat16
+I32 = mybir.dt.int32
+U32 = mybir.dt.uint32
+U8 = mybir.dt.uint8
+FP8 = mybir.dt.float8_e4m3fn
+FP8X4 = mybir.dt.float8_e4m3fn_x4
+FP4X4 = mybir.dt.float4_e2m1fn_x4
+ACT = mybir.ActivationFunctionType
+ALU = mybir.AluOpType
+
+P = 128
+B, H, C = 4, 32, 512
+EPS = 1e-5
+FLOPS = 2 * 2 * B * H * H * C * C
+
+FIRST_E = (3, 5, 7, 1)
+
+
+def tile_swintransformerblock_pb_t_w4_kernel(
+    tc,
+    o_bytes,
+    o_scale,
+    x,
+    out_w_words,
+    out_w_scales,
+    out_b,
+    norm2_w,
+    norm2_b,
+    fc1_w_words,
+    fc1_w_scales,
+    fc1_b,
+    out_x2,
+    out_g,
+):
+    nc = tc.nc
+    with ExitStack() as ctx:
+        keep = ctx.enter_context(tc.tile_pool(name="keep", bufs=1))
+        raw_pool = ctx.enter_context(tc.tile_pool(name="raw", bufs=8))
+        x_pool = ctx.enter_context(tc.tile_pool(name="xin", bufs=16))
+        two = ctx.enter_context(tc.tile_pool(name="two", bufs=2))
+        three = ctx.enter_context(tc.tile_pool(name="three", bufs=3))
+        four = ctx.enter_context(tc.tile_pool(name="four", bufs=4))
+        psum = ctx.enter_context(tc.psum_pool(name="psum", bufs=2))
+
+        warm = keep.tile([P, 1], F32)
+        nc.vector.memset(warm[:], 0.0)
+        warm_out = keep.tile([P, 1], F32)
+        nc.scalar.activation(out=warm_out[:], in_=warm[:], func=ACT.Gelu)
+
+        scale = keep.tile([P, 8], F32)
+        scale_row = o_scale.rearrange("o a u v -> (o a u v)")
+        for h in range(2):
+            nc.sync.dma_start(
+                out=scale[h:P:2, :],
+                in_=scale_row[8 * h : 8 * h + 8].partition_broadcast(64),
+            )
+
+        raws = []
+        o_rows = o_bytes.rearrange("n (h a) s d -> (n h) a (s d)", h=2)
+        for a in range(8):
+            raw = raw_pool.tile([P, 2048], U8, align_bytes=64)
+            nc.sync.dma_start(out=raw[:], in_=o_rows[:, a, :])
+            raws.append(raw)
+
+        ident = keep.tile([P, P], F32)
+        make_identity(nc, ident[:])
+
+        wz = keep.tile([P, 4, 1024], U8, align_bytes=64)
+        wzs = keep.tile([P, 4, 512], U8, align_bytes=64)
+        wf = keep.tile([P, 1024], U8, align_bytes=64)
+        wfs = keep.tile([P, 512], U8, align_bytes=64)
+        nc.gpsimd.memset(wzs[:].rearrange("p w n -> p (w n)").bitcast(I32), 0)
+        nc.gpsimd.memset(wz[:].rearrange("p w n -> p (w n)").bitcast(I32), 0)
+        nc.gpsimd.memset(wfs[:].bitcast(I32), 0)
+        half = keep.tile([P, 2], F32)
+        nc.gpsimd.memset(half[:], -0.5)
+
+        ob_bc = keep.tile([P, C], BF16)
+        nc.scalar.dma_start(out=ob_bc[:], in_=out_b.partition_broadcast(P))
+        nw_b = keep.tile([P, 4], BF16)
+        nb_b = keep.tile([P, 4], BF16)
+        nc.scalar.dma_start(out=nw_b[:], in_=norm2_w.rearrange("(p t) -> p t", t=4))
+        nc.scalar.dma_start(out=nb_b[:], in_=norm2_b.rearrange("(p t) -> p t", t=4))
+        fb_bc = keep.tile([P, C], BF16)
+        nc.scalar.dma_start(out=fb_bc[:], in_=fc1_b.partition_broadcast(P))
+
+        x_tok = x.rearrange("b (p e) c -> b p e c", e=8)
+        x_img = x.rearrange("b (i j) c -> b i j c", j=H)
+
+        xts = {}
+
+        def load_x(cp, b):
+            xt = x_pool.tile([P, 2, C], BF16)
+            xts[(cp, b)] = xt
+            e = FIRST_E[cp]
+            if cp == 2:
+                nc.sync.dma_start(out=xt[:, 0, :], in_=x_tok[b, :, e, :])
+                for w in range(4):
+                    nc.sync.dma_start(
+                        out=xt[w:P:4, 1, :], in_=x_img[b, :, 8 * ((w + 1) % 4), :]
+                    )
+            else:
+                nc.sync.dma_start(out=xt[:], in_=x_tok[b, :, e : e + 2, :])
+
+        load_x(0, 0)
+        words_i = out_w_words.bitcast(I32).rearrange("g (h p) w -> p (g h) w", h=2)
+        scales_i = out_w_scales.bitcast(I32).rearrange(
+            "g (h s q) n -> s q (g h) n", h=2, s=2
+        )
+        wzs_i = wzs[:].bitcast(I32)
+        wz_i = wz[:].bitcast(I32)
+        for c in range(2):
+            for s in range(2):
+                r0 = 32 * (2 * c + s)
+                nc.sync.dma_start(
+                    out=wzs_i[r0 : r0 + 4, 2 * c : 2 * c + 2, :], in_=scales_i[s]
+                )
+        for c in range(2):
+            nc.sync.dma_start(
+                out=wz_i[64 * c : 64 * c + 64, 2 * c : 2 * c + 2, :], in_=words_i
+            )
+        for b in range(1, B):
+            load_x(0, b)
+        for q in range(4):
+            nc.sync.dma_start(
+                out=wfs[32 * q : 32 * q + 4, :].bitcast(I32),
+                in_=fc1_w_scales[0, 4 * q : 4 * q + 4, :].bitcast(I32),
+            )
+        nc.sync.dma_start(out=wf[:].bitcast(I32), in_=fc1_w_words[0].bitcast(I32))
+
+        obs = []
+        for rh in range(2):
+            ob = keep.tile([P, 32, 8, 32], BF16, name="ob%d" % rh)
+            obs.append(ob)
+        for rh in range(2):
+            for a in range(8):
+                nc.vector.tensor_scalar(
+                    out=obs[rh][:, :, a, :],
+                    in0=raws[a][:, 1024 * rh : 1024 * rh + 1024]
+                    .bitcast(FP8)
+                    .rearrange("p (s d) -> p s d", d=32),
+                    scalar1=scale[:, a : a + 1],
+                    scalar2=None,
+                    op0=ALU.mult,
+                )
+
+        perms = {}
+        p00 = keep.tile([P, P], F32)
+        nc.scalar.copy(
+            out=p00[:].rearrange("q (b a k) -> q b a k", b=4, a=2),
+            in_=ident[:].rearrange("q (b k a) -> q b a k", b=4, a=2),
+        )
+        p10 = keep.tile([P, P], F32)
+        d10 = p10[:].rearrange("q (g k) -> q g k", k=16)
+        s00 = p00[:].rearrange("q (g k) -> q g k", k=16)
+        nc.scalar.copy(out=d10[:, :, 4:16], in_=s00[:, :, 0:12])
+        nc.scalar.copy(out=d10[:, :, 0:4], in_=s00[:, :, 12:16])
+        perms[(0, 0)] = p00
+        perms[(1, 0)] = p10
+        for rot in range(2):
+            pr = keep.tile([P, P], F32, name="perm%d" % rot)
+            d = pr[:].rearrange("q (g j) -> q g j", j=4)
+            s = perms[(rot, 0)][:].rearrange("q (g j) -> q g j", j=4)
+            nc.scalar.copy(out=d[:, :, 1:4], in_=s[:, :, 0:3])
+            nc.scalar.copy(out=d[:, :, 0:1], in_=s[:, :, 3:4])
+            perms[(rot, 1)] = pr
+
+        nw = keep.tile([P, 4], F32)
+        nb = keep.tile([P, 4], F32)
+        nc.gpsimd.tensor_copy(out=nw[:], in_=nw_b[:])
+        nc.gpsimd.tensor_copy(out=nb[:], in_=nb_b[:])
+
+        mints = {}
+
+        def turn(cp, rp):
+            if rp == 0:
+                mint = three.tile([P, 4096], BF16, align_bytes=64)
+                mints[cp] = mint
+            mint = mints[cp]
+            pt = psum.tile([P, 2, 2, P], F32)
+            words = mint[:].bitcast(F32).rearrange(
+                "p (g h j u) -> p g h j u", h=8, j=4, u=2
+            )
+            for k in range(2):
+                r = 2 * rp + k
+                src = (
+                    obs[r // 4][:]
+                    .rearrange("p s a d -> p (s a d)")
+                    .bitcast(F32)
+                )
+                w0 = ((r % 4) * 8 + 2 * cp) * 128
+                perm = perms[(1 if r >= 5 else 0, 1 if cp == 3 else 0)]
+                for u in range(2):
+                    nc.tensor.transpose(
+                        pt[:, k, u, :], src[:, w0 + u : w0 + 256 : 2], perm[:]
+                    )
+            for k in range(2):
+                rho = (2 * rp + k + 3) % 8
+                nc.scalar.copy(
+                    out=words[:, :, rho, :, :],
+                    in_=pt[:, k, :, :].rearrange("p u (g j) -> p g j u", j=4),
+                )
+
+        st = {}
+
+        def add_bias(k):
+            cp, b = divmod(k, 4)
+            xb = four.tile([P, 2, C], F32)
+            st[("xb", k)] = xb
+            for c in range(2):
+                eng = nc.vector if k < 2 else nc.gpsimd
+                eng.tensor_tensor(
+                    out=xb[:, c, :], in0=xts[(cp, b)][:, c, :], in1=ob_bc[:], op=ALU.add
+                )
+
+        def first_matmul(k):
+            cp, b = divmod(k, 4)
+            codes = three.tile([P, 256], U32, align_bytes=64)
+            planes = three.tile([P, 256], U8, align_bytes=64)
+            nc.vector.quantize_mx(
+                out=codes[:].bitcast(FP8X4),
+                scales=planes[:],
+                in_=mints[cp][:, 1024 * b : 1024 * b + 1024],
+            )
+            for c in range(2):
+                py = psum.tile([P, C], F32)
+                st[("py", k, c)] = py
+                for ah in range(2):
+                    cols = slice(128 * ah, 128 * ah + 128)
+                    nc.tensor.matmul_mx(
+                        out=py[:],
+                        lhsT=codes[:, cols].bitcast(FP8X4),
+                        lhsT_scale=planes[:, cols],
+                        rhs=wz[:, 2 * c + ah, :].bitcast(FP4X4),
+                        rhs_scale=wzs[:, 2 * c + ah, :],
+                        start=(ah == 0),
+                        stop=(ah == 1),
+                    )
+
+        x2_tok = out_x2.rearrange("b (p e) c -> b p e c", e=8)
+        x2_img = out_x2.rearrange("b (i j) c -> b i j c", j=H)
+        g_tok = out_g.rearrange("b (p e) c -> b p e c", e=8)
+        g_img = out_g.rearrange("b (i j) c -> b i j c", j=H)
+
+        def store(k, tok, img, t):
+            cp, b = divmod(k, 4)
+            e = FIRST_E[cp]
+            if cp == 2:
+                nc.sync.dma_start(out=tok[b, :, e, :], in_=t[:, 0, :])
+                for w in range(4):
+                    nc.sync.dma_start(
+                        out=img[b, :, 8 * ((w + 1) % 4), :], in_=t[w:P:4, 1, :]
+                    )
+            else:
+                nc.sync.dma_start(out=tok[b, :, e : e + 2, :], in_=t[:])
+
+        def residual(k):
+            x2 = four.tile([P, 2, C], F32)
+            st[("x2", k)] = x2
+            sums = four.tile([P, 2], F32)
+            ssq = four.tile([P, 2], F32)
+            junk = two.tile([P, C], BF16)
+            xb = st[("xb", k)]
+            for c in range(2):
+                nc.vector.scalar_tensor_tensor(
+                    out=x2[:, c, :],
+                    in0=st[("py", k, c)][:],
+                    scalar=0.0,
+                    in1=xb[:, c, :],
+                    op0=ALU.add,
+                    op1=ALU.add,
+                    accum_out=sums[:, c : c + 1],
+                )
+                nc.scalar.activation(
+                    out=junk[:],
+                    in_=x2[:, c, :],
+                    func=ACT.Square,
+                    bias=sums[:, c : c + 1],
+                    scale=-512.0,
+                    accum_out=ssq[:, c : c + 1],
+                )
+            nm = four.tile([P, 2], F32)
+            var = four.tile([P, 2], F32)
+            rstd = four.tile([P, 2], F32)
+            nc.gpsimd.tensor_scalar(
+                out=nm[:], in0=sums[:], scalar1=-1.0 / 512, scalar2=0.0, op0=ALU.mult, op1=ALU.add
+            )
+            nc.gpsimd.tensor_scalar(
+                out=var[:], in0=ssq[:], scalar1=2.0**-27, scalar2=EPS, op0=ALU.mult, op1=ALU.add
+            )
+            nc.gpsimd.tensor_tensor(out=rstd[:], in0=var[:], in1=half[:], op=ALU.pow)
+            st[("nm", k)] = nm
+            st[("rstd", k)] = rstd
+            store(k, x2_tok, x2_img, x2)
+
+        def normalise(k):
+            z = two.tile([P, 2, 4, P], F32)
+            x2 = st[("x2", k)]
+            for c in range(2):
+                nc.vector.tensor_scalar(
+                    out=z[:, c, :, :],
+                    in0=x2[:, c, :].rearrange("q (p t) -> q t p", t=4),
+                    scalar1=st[("nm", k)][:, c : c + 1],
+                    scalar2=st[("rstd", k)][:, c : c + 1],
+                    op0=ALU.add,
+                    op1=ALU.mult,
+                )
+            hp = two.tile([P, 4, 256], BF16)
+            st[("hp", k)] = hp
+            for th in range(2):
+                pz = psum.tile([P, 2, 256], F32)
+                for t in range(2):
+                    for c in range(2):
+                        nc.tensor.transpose(
+                            pz[:, t, 128 * c : 128 * c + 128], z[:, c, 2 * th + t, :], ident[:]
+                        )
+                for t in range(2):
+                    j = 2 * th + t
+                    nc.scalar.activation(
+                        out=hp[:, j, :],
+                        in_=pz[:, t, :],
+                        func=ACT.Identity,
+                        bias=nb[:, j : j + 1],
+                        scale=nw[:, j : j + 1],
+                    )
+
+        def second_matmul(k):
+            hi = two.tile([P, 256, 4], BF16, align_bytes=64)
+            nc.vector.tensor_copy(out=hi[:], in_=st[("hp", k)][:].rearrange("p t n -> p n t"))
+            codes2 = three.tile([P, 256], U32, align_bytes=64)
+            planes2 = three.tile([P, 256], U8, align_bytes=64)
+            nc.vector.quantize_mx(
+                out=codes2[:].bitcast(FP8X4),
+                scales=planes2[:],
+                in_=hi[:].rearrange("p n t -> p (n t)"),
+            )
+            for c in range(2):
+                pv = psum.tile([P, C], F32)
+                st[("pv", k, c)] = pv
+                cols = slice(128 * c, 128 * c + 128)
+                nc.tensor.matmul_mx(
+                    out=pv[:],
+                    lhsT=codes2[:, cols].bitcast(FP8X4),
+                    lhsT_scale=planes2[:, cols],
+                    rhs=wf[:].bitcast(FP4X4),
+                    rhs_scale=wfs[:],
+                    start=True,
+                    stop=True,
+                )
+
+        def finish(k):
+            v = two.tile([P, 2, C], F32)
+            for c in range(2):
+                nc.vector.tensor_tensor(
+                    out=v[:, c, :], in0=st[("pv", k, c)][:], in1=fb_bc[:], op=ALU.add
+                )
+            g = three.tile([P, 2, C], F32)
+            nc.scalar.activation(out=g[:], in_=v[:], func=ACT.Gelu)
+            store(k, g_tok, g_img, g)
+
+        ctx.enter_context(tc.manual_schedule())
+        steps = 16
+        def add_turn(n):
+            cp, rp = divmod(n, 4)
+            if cp < 4:
+                turn(cp, rp)
+
+        for n in range(5):
+            add_turn(n)
+        for k in range(2):
+            add_bias(k)
+        for i in range(steps + 4):
+            if 4 <= i + 3 < steps:
+                load_x((i + 3) // 4, (i + 3) % 4)
+            if i + 2 < steps:
+                add_bias(i + 2)
+            if i < steps:
+                first_matmul(i)
+            if 0 <= i - 4:
+                finish(i - 4)
+            if 0 <= i - 1 < steps:
+                residual(i - 1)
+            if 0 <= i - 3 < steps:
+                second_matmul(i - 3)
+            if 0 <= i - 2 < steps:
+                normalise(i - 2)
+            add_turn(i + 5)

@@ -21,6 +21,35 @@ FLOPS = 2 * 2 * B * H * H * C * C
 
 FIRST_E = (3, 5, 7, 1)
 
+ZDVE = ()
+BPOOL = ()
+ORDER = (
+    ("R", -5),
+    ("B0", 0),
+    ("Q", 0),
+    ("C", -5),
+    ("N0", 2),
+    ("A0", 1),
+    ("N1", 2),
+    ("A1", 1),
+    ("S0", 1),
+    ("S1", 1),
+    ("G0", 4),
+    ("V", 1),
+    ("I", 3),
+    ("B1", 0),
+    ("M", 0),
+    ("U", 5),
+    ("T0", 2),
+    ("H", 3),
+    ("E0", 2),
+    ("T1", 2),
+    ("E1", 2),
+    ("K", 3),
+    ("X", -4),
+    ("G1", 4),
+)
+
 
 def tile_swintransformerblock_pb_t_w4_kernel(
     tc,
@@ -46,6 +75,7 @@ def tile_swintransformerblock_pb_t_w4_kernel(
         two = ctx.enter_context(tc.tile_pool(name="two", bufs=2))
         three = ctx.enter_context(tc.tile_pool(name="three", bufs=3))
         four = ctx.enter_context(tc.tile_pool(name="four", bufs=4))
+        xb_pool = ctx.enter_context(tc.tile_pool(name="xb", bufs=4))
         psum = ctx.enter_context(tc.psum_pool(name="psum", bufs=2))
 
         warm = keep.tile([P, 1], F32)
@@ -177,6 +207,7 @@ def tile_swintransformerblock_pb_t_w4_kernel(
         nc.gpsimd.tensor_copy(out=nb[:], in_=nb_b[:])
 
         mints = {}
+        st = {}
 
         def turn(cp, rp):
             if rp == 0:
@@ -184,9 +215,6 @@ def tile_swintransformerblock_pb_t_w4_kernel(
                 mints[cp] = mint
             mint = mints[cp]
             pt = psum.tile([P, 2, 2, P], F32)
-            words = mint[:].bitcast(F32).rearrange(
-                "p (g h j u) -> p g h j u", h=8, j=4, u=2
-            )
             for k in range(2):
                 r = 2 * rp + k
                 src = (
@@ -200,6 +228,13 @@ def tile_swintransformerblock_pb_t_w4_kernel(
                     nc.tensor.transpose(
                         pt[:, k, u, :], src[:, w0 + u : w0 + 256 : 2], perm[:]
                     )
+            st[("pt", cp, rp)] = pt
+
+        def turn_out(cp, rp):
+            pt = st[("pt", cp, rp)]
+            words = mints[cp][:].bitcast(F32).rearrange(
+                "p (g h j u) -> p g h j u", h=8, j=4, u=2
+            )
             for k in range(2):
                 rho = (2 * rp + k + 3) % 8
                 nc.scalar.copy(
@@ -207,19 +242,16 @@ def tile_swintransformerblock_pb_t_w4_kernel(
                     in_=pt[:, k, :, :].rearrange("p u (g j) -> p g j u", j=4),
                 )
 
-        st = {}
-
-        def add_bias(k):
+        def add_bias(k, c):
             cp, b = divmod(k, 4)
-            xb = four.tile([P, 2, C], F32)
-            st[("xb", k)] = xb
-            for c in range(2):
-                eng = nc.vector if k < 2 else nc.gpsimd
-                eng.tensor_tensor(
-                    out=xb[:, c, :], in0=xts[(cp, b)][:, c, :], in1=ob_bc[:], op=ALU.add
-                )
+            if c == 0:
+                st[("xb", k)] = xb_pool.tile([P, 2, C], F32, name="xb")
+            eng = nc.gpsimd if (2 * k + c) in BPOOL else nc.vector
+            eng.tensor_tensor(
+                out=st[("xb", k)][:, c, :], in0=xts[(cp, b)][:, c, :], in1=ob_bc[:], op=ALU.add
+            )
 
-        def first_matmul(k):
+        def quantise_m(k):
             cp, b = divmod(k, 4)
             codes = three.tile([P, 256], U32, align_bytes=64)
             planes = three.tile([P, 256], U8, align_bytes=64)
@@ -228,6 +260,10 @@ def tile_swintransformerblock_pb_t_w4_kernel(
                 scales=planes[:],
                 in_=mints[cp][:, 1024 * b : 1024 * b + 1024],
             )
+            st[("q1", k)] = (codes, planes)
+
+        def first_matmul(k):
+            codes, planes = st[("q1", k)]
             for c in range(2):
                 py = psum.tile([P, C], F32)
                 st[("py", k, c)] = py
@@ -260,86 +296,120 @@ def tile_swintransformerblock_pb_t_w4_kernel(
             else:
                 nc.sync.dma_start(out=tok[b, :, e : e + 2, :], in_=t[:])
 
-        def residual(k):
-            x2 = four.tile([P, 2, C], F32)
-            st[("x2", k)] = x2
-            sums = four.tile([P, 2], F32)
-            ssq = four.tile([P, 2], F32)
+        def residual(k, c):
+            if c == 0:
+                st[("x2", k)] = four.tile([P, 2, C], F32, name="x2")
+                st[("sums", k)] = four.tile([P, 2], F32, name="sums")
+                st[("ssq", k)] = four.tile([P, 2], F32, name="ssq")
+            nc.vector.scalar_tensor_tensor(
+                out=st[("x2", k)][:, c, :],
+                in0=st[("py", k, c)][:],
+                scalar=0.0,
+                in1=st[("xb", k)][:, c, :],
+                op0=ALU.add,
+                op1=ALU.add,
+                accum_out=st[("sums", k)][:, c : c + 1],
+            )
+
+        def squares(k, c):
             junk = two.tile([P, C], BF16)
-            xb = st[("xb", k)]
-            for c in range(2):
-                nc.vector.scalar_tensor_tensor(
-                    out=x2[:, c, :],
-                    in0=st[("py", k, c)][:],
-                    scalar=0.0,
-                    in1=xb[:, c, :],
-                    op0=ALU.add,
-                    op1=ALU.add,
-                    accum_out=sums[:, c : c + 1],
-                )
-                nc.scalar.activation(
-                    out=junk[:],
-                    in_=x2[:, c, :],
-                    func=ACT.Square,
-                    bias=sums[:, c : c + 1],
-                    scale=-512.0,
-                    accum_out=ssq[:, c : c + 1],
-                )
+            nc.scalar.activation(
+                out=junk[:],
+                in_=st[("x2", k)][:, c, :],
+                func=ACT.Square,
+                bias=st[("sums", k)][:, c : c + 1],
+                scale=-512.0,
+                accum_out=st[("ssq", k)][:, c : c + 1],
+            )
+
+        def statistics(k):
             nm = four.tile([P, 2], F32)
             var = four.tile([P, 2], F32)
             rstd = four.tile([P, 2], F32)
+            nmr = four.tile([P, 2], F32)
             nc.gpsimd.tensor_scalar(
-                out=nm[:], in0=sums[:], scalar1=-1.0 / 512, scalar2=0.0, op0=ALU.mult, op1=ALU.add
+                out=nm[:],
+                in0=st[("sums", k)][:],
+                scalar1=-1.0 / 512,
+                scalar2=0.0,
+                op0=ALU.mult,
+                op1=ALU.add,
             )
             nc.gpsimd.tensor_scalar(
-                out=var[:], in0=ssq[:], scalar1=2.0**-27, scalar2=EPS, op0=ALU.mult, op1=ALU.add
+                out=var[:],
+                in0=st[("ssq", k)][:],
+                scalar1=2.0**-27,
+                scalar2=EPS,
+                op0=ALU.mult,
+                op1=ALU.add,
             )
             nc.gpsimd.tensor_tensor(out=rstd[:], in0=var[:], in1=half[:], op=ALU.pow)
-            st[("nm", k)] = nm
+            nc.gpsimd.tensor_tensor(out=nmr[:], in0=nm[:], in1=rstd[:], op=ALU.mult)
             st[("rstd", k)] = rstd
-            store(k, x2_tok, x2_img, x2)
+            st[("nmr", k)] = nmr
+            store(k, x2_tok, x2_img, st[("x2", k)])
 
-        def normalise(k):
-            z = two.tile([P, 2, 4, P], F32)
-            x2 = st[("x2", k)]
-            for c in range(2):
+        def normalise(k, c):
+            if c == 0:
+                st[("z", k)] = two.tile([P, 2, 4, P], F32, name="z")
+            z = st[("z", k)]
+            src = st[("x2", k)][:, c, :].rearrange("q (p t) -> q t p", t=4)
+            rstd = st[("rstd", k)][:, c : c + 1]
+            nmr = st[("nmr", k)][:, c : c + 1]
+            if (2 * k + c) in ZDVE:
                 nc.vector.tensor_scalar(
                     out=z[:, c, :, :],
-                    in0=x2[:, c, :].rearrange("q (p t) -> q t p", t=4),
-                    scalar1=st[("nm", k)][:, c : c + 1],
-                    scalar2=st[("rstd", k)][:, c : c + 1],
-                    op0=ALU.add,
-                    op1=ALU.mult,
+                    in0=src,
+                    scalar1=rstd,
+                    scalar2=nmr,
+                    op0=ALU.mult,
+                    op1=ALU.add,
                 )
-            hp = two.tile([P, 4, 256], BF16)
-            st[("hp", k)] = hp
-            for th in range(2):
-                pz = psum.tile([P, 2, 256], F32)
-                for t in range(2):
-                    for c in range(2):
-                        nc.tensor.transpose(
-                            pz[:, t, 128 * c : 128 * c + 128], z[:, c, 2 * th + t, :], ident[:]
-                        )
-                for t in range(2):
-                    j = 2 * th + t
-                    nc.scalar.activation(
-                        out=hp[:, j, :],
-                        in_=pz[:, t, :],
-                        func=ACT.Identity,
-                        bias=nb[:, j : j + 1],
-                        scale=nw[:, j : j + 1],
+            else:
+                nc.scalar.activation(
+                    out=z[:, c, :, :], in_=src, func=ACT.Identity, bias=nmr, scale=rstd
+                )
+
+        def turn_z(k, th):
+            z = st[("z", k)]
+            pz = psum.tile([P, 2, 256], F32)
+            st[("pz", k, th)] = pz
+            for t in range(2):
+                for c in range(2):
+                    nc.tensor.transpose(
+                        pz[:, t, 128 * c : 128 * c + 128], z[:, c, 2 * th + t, :], ident[:]
                     )
 
-        def second_matmul(k):
+        def affine(k, th):
+            if th == 0:
+                st[("hp", k)] = two.tile([P, 4, 256], BF16, name="hp")
+            for t in range(2):
+                j = 2 * th + t
+                nc.scalar.activation(
+                    out=st[("hp", k)][:, j, :],
+                    in_=st[("pz", k, th)][:, t, :],
+                    func=ACT.Identity,
+                    bias=nb[:, j : j + 1],
+                    scale=nw[:, j : j + 1],
+                )
+
+        def interleave(k):
             hi = two.tile([P, 256, 4], BF16, align_bytes=64)
+            st[("hi", k)] = hi
             nc.vector.tensor_copy(out=hi[:], in_=st[("hp", k)][:].rearrange("p t n -> p n t"))
+
+        def quantise_h(k):
             codes2 = three.tile([P, 256], U32, align_bytes=64)
             planes2 = three.tile([P, 256], U8, align_bytes=64)
             nc.vector.quantize_mx(
                 out=codes2[:].bitcast(FP8X4),
                 scales=planes2[:],
-                in_=hi[:].rearrange("p n t -> p (n t)"),
+                in_=st[("hi", k)][:].rearrange("p n t -> p (n t)"),
             )
+            st[("q2", k)] = (codes2, planes2)
+
+        def second_matmul(k):
+            codes2, planes2 = st[("q2", k)]
             for c in range(2):
                 pv = psum.tile([P, C], F32)
                 st[("pv", k, c)] = pv
@@ -354,40 +424,48 @@ def tile_swintransformerblock_pb_t_w4_kernel(
                     stop=True,
                 )
 
-        def finish(k):
-            v = two.tile([P, 2, C], F32)
-            for c in range(2):
-                nc.vector.tensor_tensor(
-                    out=v[:, c, :], in0=st[("pv", k, c)][:], in1=fb_bc[:], op=ALU.add
-                )
+        def bias_g(k, c):
+            if c == 0:
+                st[("v", k)] = two.tile([P, 2, C], F32, name="v")
+            nc.vector.tensor_tensor(
+                out=st[("v", k)][:, c, :], in0=st[("pv", k, c)][:], in1=fb_bc[:], op=ALU.add
+            )
+
+        def gelu(k):
             g = three.tile([P, 2, C], F32)
-            nc.scalar.activation(out=g[:], in_=v[:], func=ACT.Gelu)
+            nc.scalar.activation(out=g[:], in_=st[("v", k)][:], func=ACT.Gelu)
             store(k, g_tok, g_img, g)
 
         ctx.enter_context(tc.manual_schedule())
-        steps = 16
-        def add_turn(n):
-            cp, rp = divmod(n, 4)
-            if cp < 4:
-                turn(cp, rp)
-
-        for n in range(5):
-            add_turn(n)
-        for k in range(2):
-            add_bias(k)
-        for i in range(steps + 4):
-            if 4 <= i + 3 < steps:
-                load_x((i + 3) // 4, (i + 3) % 4)
-            if i + 2 < steps:
-                add_bias(i + 2)
-            if i < steps:
-                first_matmul(i)
-            if 0 <= i - 4:
-                finish(i - 4)
-            if 0 <= i - 1 < steps:
-                residual(i - 1)
-            if 0 <= i - 3 < steps:
-                second_matmul(i - 3)
-            if 0 <= i - 2 < steps:
-                normalise(i - 2)
-            add_turn(i + 5)
+        actions = {
+            "X": lambda k: load_x(k // 4, k % 4) if k >= 4 else None,
+            "B0": lambda k: add_bias(k, 0),
+            "B1": lambda k: add_bias(k, 1),
+            "Q": quantise_m,
+            "M": first_matmul,
+            "A0": lambda k: residual(k, 0),
+            "A1": lambda k: residual(k, 1),
+            "S0": lambda k: squares(k, 0),
+            "S1": lambda k: squares(k, 1),
+            "V": statistics,
+            "N0": lambda k: normalise(k, 0),
+            "N1": lambda k: normalise(k, 1),
+            "T0": lambda k: turn_z(k, 0),
+            "T1": lambda k: turn_z(k, 1),
+            "E0": lambda k: affine(k, 0),
+            "E1": lambda k: affine(k, 1),
+            "I": interleave,
+            "H": quantise_h,
+            "K": second_matmul,
+            "G0": lambda k: bias_g(k, 0),
+            "G1": lambda k: bias_g(k, 1),
+            "U": gelu,
+            "R": lambda k: turn(k // 4, k % 4),
+            "C": lambda k: turn_out(k // 4, k % 4),
+        }
+        lead = max(-lag for action, lag in ORDER)
+        trail = max(lag for action, lag in ORDER)
+        for i in range(-lead, 16 + trail):
+            for action, lag in ORDER:
+                if 0 <= i - lag < 16:
+                    actions[action](i - lag)

@@ -22,32 +22,31 @@ FLOPS = 2 * 2 * B * H * H * C * C
 FIRST_E = (3, 5, 7, 1)
 
 ZDVE = ()
-BPOOL = ()
+HEAT = 1
 ORDER = (
-    ("R", -5),
-    ("B0", 0),
+    ("X", -3),
     ("Q", 0),
-    ("C", -5),
+    ("M", 0),
     ("N0", 2),
+    ("G1", 5),
     ("A0", 1),
     ("N1", 2),
     ("A1", 1),
+    ("G0", 4),
+    ("I", 3),
+    ("B", -2),
+    ("H", 3),
     ("S0", 1),
     ("S1", 1),
-    ("G0", 4),
-    ("V", 1),
-    ("I", 3),
-    ("B1", 0),
-    ("M", 0),
-    ("U", 5),
     ("T0", 2),
-    ("H", 3),
+    ("V", 1),
+    ("U", 5),
     ("E0", 2),
     ("T1", 2),
     ("E1", 2),
+    ("R", -6),
+    ("C", -6),
     ("K", 3),
-    ("X", -4),
-    ("G1", 4),
 )
 
 
@@ -242,13 +241,14 @@ def tile_swintransformerblock_pb_t_w4_kernel(
                     in_=pt[:, k, :, :].rearrange("p u (g j) -> p g j u", j=4),
                 )
 
-        def add_bias(k, c):
-            cp, b = divmod(k, 4)
-            if c == 0:
-                st[("xb", k)] = xb_pool.tile([P, 2, C], F32, name="xb")
-            eng = nc.gpsimd if (2 * k + c) in BPOOL else nc.vector
-            eng.tensor_tensor(
-                out=st[("xb", k)][:, c, :], in0=xts[(cp, b)][:, c, :], in1=ob_bc[:], op=ALU.add
+        def add_bias(k):
+            xb = xb_pool.tile([P, 2, C], F32)
+            st[("xb", k)] = xb
+            nc.vector.tensor_tensor(
+                out=xb[:],
+                in0=xts[divmod(k, 4)][:],
+                in1=ob_bc[:].unsqueeze(1).to_broadcast([P, 2, C]),
+                op=ALU.add,
             )
 
         def quantise_m(k):
@@ -267,6 +267,16 @@ def tile_swintransformerblock_pb_t_w4_kernel(
             for c in range(2):
                 py = psum.tile([P, C], F32)
                 st[("py", k, c)] = py
+                for warm_up in range(HEAT):
+                    nc.tensor.matmul_mx(
+                        out=py[:],
+                        lhsT=codes[:, 0:128].bitcast(FP8X4),
+                        lhsT_scale=planes[:, 0:128],
+                        rhs=wz[:, 2 * c, :].bitcast(FP4X4),
+                        rhs_scale=wzs[:, 2 * c, :],
+                        start=True,
+                        stop=True,
+                    )
                 for ah in range(2):
                     cols = slice(128 * ah, 128 * ah + 128)
                     nc.tensor.matmul_mx(
@@ -351,14 +361,14 @@ def tile_swintransformerblock_pb_t_w4_kernel(
 
         def normalise(k, c):
             if c == 0:
-                st[("z", k)] = two.tile([P, 2, 4, P], F32, name="z")
+                st[("z", k)] = two.tile([P, 2, C], F32, name="z")
             z = st[("z", k)]
-            src = st[("x2", k)][:, c, :].rearrange("q (p t) -> q t p", t=4)
+            src = st[("x2", k)][:, c, :]
             rstd = st[("rstd", k)][:, c : c + 1]
             nmr = st[("nmr", k)][:, c : c + 1]
             if (2 * k + c) in ZDVE:
                 nc.vector.tensor_scalar(
-                    out=z[:, c, :, :],
+                    out=z[:, c, :],
                     in0=src,
                     scalar1=rstd,
                     scalar2=nmr,
@@ -367,7 +377,7 @@ def tile_swintransformerblock_pb_t_w4_kernel(
                 )
             else:
                 nc.scalar.activation(
-                    out=z[:, c, :, :], in_=src, func=ACT.Identity, bias=nmr, scale=rstd
+                    out=z[:, c, :], in_=src, func=ACT.Identity, bias=nmr, scale=rstd
                 )
 
         def turn_z(k, th):
@@ -377,7 +387,7 @@ def tile_swintransformerblock_pb_t_w4_kernel(
             for t in range(2):
                 for c in range(2):
                     nc.tensor.transpose(
-                        pz[:, t, 128 * c : 128 * c + 128], z[:, c, 2 * th + t, :], ident[:]
+                        pz[:, t, 128 * c : 128 * c + 128], z[:, c, 2 * th + t : C : 4], ident[:]
                     )
 
         def affine(k, th):
@@ -439,8 +449,7 @@ def tile_swintransformerblock_pb_t_w4_kernel(
         ctx.enter_context(tc.manual_schedule())
         actions = {
             "X": lambda k: load_x(k // 4, k % 4) if k >= 4 else None,
-            "B0": lambda k: add_bias(k, 0),
-            "B1": lambda k: add_bias(k, 1),
+            "B": add_bias,
             "Q": quantise_m,
             "M": first_matmul,
             "A0": lambda k: residual(k, 0),

@@ -21,32 +21,32 @@ FLOPS = 2 * 2 * B * H * H * C * C
 
 FIRST_E = (3, 5, 7, 1)
 
-ZDVE = ()
+ZDVE = (1, 2, 6, 11, 22, 24, 27, 28, 29, 30, 31)
 HEAT = 1
 ORDER = (
-    ("X", -3),
-    ("Q", 0),
+    ("V", 2),
     ("M", 0),
-    ("N0", 2),
+    ("Q", -1),
     ("G1", 5),
+    ("X", -5),
     ("A0", 1),
-    ("N1", 2),
-    ("A1", 1),
-    ("G0", 4),
-    ("I", 3),
-    ("B", -2),
-    ("H", 3),
     ("S0", 1),
-    ("S1", 1),
+    ("A1", 1),
+    ("N0", 2),
+    ("N1", 2),
     ("T0", 2),
-    ("V", 1),
+    ("S1", 1),
+    ("I", 3),
     ("U", 5),
-    ("E0", 2),
+    ("G0", 4),
+    ("B", -3),
     ("T1", 2),
-    ("E1", 2),
-    ("R", -6),
-    ("C", -6),
+    ("R", -7),
+    ("H", 3),
     ("K", 3),
+    ("E0", 2),
+    ("E1", 2),
+    ("C", -7),
 )
 
 
@@ -82,6 +82,12 @@ def tile_swintransformerblock_pb_t_w4_kernel(
         warm_out = keep.tile([P, 1], F32)
         nc.scalar.activation(out=warm_out[:], in_=warm[:], func=ACT.Gelu)
 
+        rows = keep.tile([P, 2, C], BF16)
+        nc.vector.memset(rows[:].rearrange("p v c -> p (v c)").bitcast(I32), 0)
+        ones = keep.tile([P, P], BF16)
+        nc.vector.memset(ones[:], 1.0)
+        nc.gpsimd.dma_start(out=rows[0:1, 0, :], in_=out_b.unsqueeze(0))
+        nc.gpsimd.dma_start(out=rows[0:1, 1, :], in_=fc1_b.unsqueeze(0))
         scale = keep.tile([P, 8], F32)
         scale_row = o_scale.rearrange("o a u v -> (o a u v)")
         for h in range(2):
@@ -104,20 +110,16 @@ def tile_swintransformerblock_pb_t_w4_kernel(
         wzs = keep.tile([P, 4, 512], U8, align_bytes=64)
         wf = keep.tile([P, 1024], U8, align_bytes=64)
         wfs = keep.tile([P, 512], U8, align_bytes=64)
-        nc.gpsimd.memset(wzs[:].rearrange("p w n -> p (w n)").bitcast(I32), 0)
-        nc.gpsimd.memset(wz[:].rearrange("p w n -> p (w n)").bitcast(I32), 0)
-        nc.gpsimd.memset(wfs[:].bitcast(I32), 0)
+        nc.vector.memset(wzs[:].rearrange("p w n -> p (w n)").bitcast(I32), 0)
+        nc.vector.memset(wz[:].rearrange("p w n -> p (w n)").bitcast(I32), 0)
+        nc.vector.memset(wfs[:].bitcast(I32), 0)
         half = keep.tile([P, 2], F32)
         nc.gpsimd.memset(half[:], -0.5)
 
-        ob_bc = keep.tile([P, C], BF16)
-        nc.scalar.dma_start(out=ob_bc[:], in_=out_b.partition_broadcast(P))
         nw_b = keep.tile([P, 4], BF16)
         nb_b = keep.tile([P, 4], BF16)
         nc.scalar.dma_start(out=nw_b[:], in_=norm2_w.rearrange("(p t) -> p t", t=4))
         nc.scalar.dma_start(out=nb_b[:], in_=norm2_b.rearrange("(p t) -> p t", t=4))
-        fb_bc = keep.tile([P, C], BF16)
-        nc.scalar.dma_start(out=fb_bc[:], in_=fc1_b.partition_broadcast(P))
 
         x_tok = x.rearrange("b (p e) c -> b p e c", e=8)
         x_img = x.rearrange("b (i j) c -> b i j c", j=H)
@@ -205,6 +207,14 @@ def tile_swintransformerblock_pb_t_w4_kernel(
         nc.gpsimd.tensor_copy(out=nw[:], in_=nw_b[:])
         nc.gpsimd.tensor_copy(out=nb[:], in_=nb_b[:])
 
+        spread = []
+        for v in range(2):
+            pv = psum.tile([P, C], F32)
+            nc.tensor.matmul(pv[:], lhsT=ones[:], rhs=rows[:, v, :], start=True, stop=True)
+            bc = keep.tile([P, C], BF16, name="bias%d" % v)
+            nc.scalar.copy(out=bc[:], in_=pv[:])
+            spread.append(bc)
+        ob_bc, fb_bc = spread
         mints = {}
         st = {}
 
@@ -443,8 +453,17 @@ def tile_swintransformerblock_pb_t_w4_kernel(
 
         def gelu(k):
             g = three.tile([P, 2, C], F32)
-            nc.scalar.activation(out=g[:], in_=st[("v", k)][:], func=ACT.Gelu)
-            store(k, g_tok, g_img, g)
+            if k < 15:
+                nc.scalar.activation(out=g[:], in_=st[("v", k)][:], func=ACT.Gelu)
+                store(k, g_tok, g_img, g)
+            else:
+                for c in range(2):
+                    nc.scalar.activation(
+                        out=g[:, c, :], in_=st[("v", k)][:, c, :], func=ACT.Gelu
+                    )
+                    nc.sync.dma_start(
+                        out=g_tok[3, :, FIRST_E[3] + c, :], in_=g[:, c, :]
+                    )
 
         ctx.enter_context(tc.manual_schedule())
         actions = {

from contextlib import ExitStack

import concourse.mybir as mybir
from concourse.masks import make_identity

F32 = mybir.dt.float32
BF16 = mybir.dt.bfloat16
I32 = mybir.dt.int32
U32 = mybir.dt.uint32
U8 = mybir.dt.uint8
FP8 = mybir.dt.float8_e4m3fn
FP8X4 = mybir.dt.float8_e4m3fn_x4
FP4X4 = mybir.dt.float4_e2m1fn_x4
ACT = mybir.ActivationFunctionType
ALU = mybir.AluOpType

P = 128
B, H, C = 4, 32, 512
EPS = 1e-5
FLOPS = 2 * 2 * B * H * H * C * C

FIRST_E = (3, 5, 7, 1)

ZDVE = (1, 2, 6, 11, 22, 24, 27, 28, 29, 30, 31)
HEAT = 1
ORDER = (
    ("V", 2),
    ("M", 0),
    ("Q", -1),
    ("G1", 5),
    ("X", -5),
    ("A0", 1),
    ("S0", 1),
    ("A1", 1),
    ("N0", 2),
    ("N1", 2),
    ("T0", 2),
    ("S1", 1),
    ("I", 3),
    ("U", 5),
    ("G0", 4),
    ("B", -3),
    ("T1", 2),
    ("R", -7),
    ("H", 3),
    ("K", 3),
    ("E0", 2),
    ("E1", 2),
    ("C", -7),
)


def tile_swintransformerblock_pb_t_w4_kernel(
    tc,
    o_bytes,
    o_scale,
    x,
    out_w_words,
    out_w_scales,
    out_b,
    norm2_w,
    norm2_b,
    fc1_w_words,
    fc1_w_scales,
    fc1_b,
    out_x2,
    out_g,
):
    nc = tc.nc
    with ExitStack() as ctx:
        keep = ctx.enter_context(tc.tile_pool(name="keep", bufs=1))
        raw_pool = ctx.enter_context(tc.tile_pool(name="raw", bufs=8))
        x_pool = ctx.enter_context(tc.tile_pool(name="xin", bufs=16))
        two = ctx.enter_context(tc.tile_pool(name="two", bufs=2))
        three = ctx.enter_context(tc.tile_pool(name="three", bufs=3))
        four = ctx.enter_context(tc.tile_pool(name="four", bufs=4))
        xb_pool = ctx.enter_context(tc.tile_pool(name="xb", bufs=4))
        psum = ctx.enter_context(tc.psum_pool(name="psum", bufs=2))

        warm = keep.tile([P, 1], F32)
        nc.vector.memset(warm[:], 0.0)
        warm_out = keep.tile([P, 1], F32)
        nc.scalar.activation(out=warm_out[:], in_=warm[:], func=ACT.Gelu)

        rows = keep.tile([P, 2, C], BF16)
        nc.vector.memset(rows[:].rearrange("p v c -> p (v c)").bitcast(I32), 0)
        ones = keep.tile([P, P], BF16)
        nc.vector.memset(ones[:], 1.0)
        nc.gpsimd.dma_start(out=rows[0:1, 0, :], in_=out_b.unsqueeze(0))
        nc.gpsimd.dma_start(out=rows[0:1, 1, :], in_=fc1_b.unsqueeze(0))
        scale = keep.tile([P, 8], F32)
        scale_row = o_scale.rearrange("o a u v -> (o a u v)")
        for h in range(2):
            nc.sync.dma_start(
                out=scale[h:P:2, :],
                in_=scale_row[8 * h : 8 * h + 8].partition_broadcast(64),
            )

        raws = []
        o_rows = o_bytes.rearrange("n (h a) s d -> (n h) a (s d)", h=2)
        for a in range(8):
            raw = raw_pool.tile([P, 2048], U8, align_bytes=64)
            nc.sync.dma_start(out=raw[:], in_=o_rows[:, a, :])
            raws.append(raw)

        ident = keep.tile([P, P], F32)
        make_identity(nc, ident[:])

        wz = keep.tile([P, 4, 1024], U8, align_bytes=64)
        wzs = keep.tile([P, 4, 512], U8, align_bytes=64)
        wf = keep.tile([P, 1024], U8, align_bytes=64)
        wfs = keep.tile([P, 512], U8, align_bytes=64)
        nc.vector.memset(wzs[:].rearrange("p w n -> p (w n)").bitcast(I32), 0)
        nc.vector.memset(wz[:].rearrange("p w n -> p (w n)").bitcast(I32), 0)
        nc.vector.memset(wfs[:].bitcast(I32), 0)
        half = keep.tile([P, 2], F32)
        nc.gpsimd.memset(half[:], -0.5)

        nw_b = keep.tile([P, 4], BF16)
        nb_b = keep.tile([P, 4], BF16)
        nc.scalar.dma_start(out=nw_b[:], in_=norm2_w.rearrange("(p t) -> p t", t=4))
        nc.scalar.dma_start(out=nb_b[:], in_=norm2_b.rearrange("(p t) -> p t", t=4))

        x_tok = x.rearrange("b (p e) c -> b p e c", e=8)
        x_img = x.rearrange("b (i j) c -> b i j c", j=H)

        xts = {}

        def load_x(cp, b):
            xt = x_pool.tile([P, 2, C], BF16)
            xts[(cp, b)] = xt
            e = FIRST_E[cp]
            if cp == 2:
                nc.sync.dma_start(out=xt[:, 0, :], in_=x_tok[b, :, e, :])
                for w in range(4):
                    nc.sync.dma_start(
                        out=xt[w:P:4, 1, :], in_=x_img[b, :, 8 * ((w + 1) % 4), :]
                    )
            else:
                nc.sync.dma_start(out=xt[:], in_=x_tok[b, :, e : e + 2, :])

        load_x(0, 0)
        words_i = out_w_words.bitcast(I32).rearrange("g (h p) w -> p (g h) w", h=2)
        scales_i = out_w_scales.bitcast(I32).rearrange(
            "g (h s q) n -> s q (g h) n", h=2, s=2
        )
        wzs_i = wzs[:].bitcast(I32)
        wz_i = wz[:].bitcast(I32)
        for c in range(2):
            for s in range(2):
                r0 = 32 * (2 * c + s)
                nc.sync.dma_start(
                    out=wzs_i[r0 : r0 + 4, 2 * c : 2 * c + 2, :], in_=scales_i[s]
                )
        for c in range(2):
            nc.sync.dma_start(
                out=wz_i[64 * c : 64 * c + 64, 2 * c : 2 * c + 2, :], in_=words_i
            )
        for b in range(1, B):
            load_x(0, b)
        for q in range(4):
            nc.sync.dma_start(
                out=wfs[32 * q : 32 * q + 4, :].bitcast(I32),
                in_=fc1_w_scales[0, 4 * q : 4 * q + 4, :].bitcast(I32),
            )
        nc.sync.dma_start(out=wf[:].bitcast(I32), in_=fc1_w_words[0].bitcast(I32))

        obs = []
        for rh in range(2):
            ob = keep.tile([P, 32, 8, 32], BF16, name="ob%d" % rh)
            obs.append(ob)
        for rh in range(2):
            for a in range(8):
                nc.vector.tensor_scalar(
                    out=obs[rh][:, :, a, :],
                    in0=raws[a][:, 1024 * rh : 1024 * rh + 1024]
                    .bitcast(FP8)
                    .rearrange("p (s d) -> p s d", d=32),
                    scalar1=scale[:, a : a + 1],
                    scalar2=None,
                    op0=ALU.mult,
                )

        perms = {}
        p00 = keep.tile([P, P], F32)
        nc.scalar.copy(
            out=p00[:].rearrange("q (b a k) -> q b a k", b=4, a=2),
            in_=ident[:].rearrange("q (b k a) -> q b a k", b=4, a=2),
        )
        p10 = keep.tile([P, P], F32)
        d10 = p10[:].rearrange("q (g k) -> q g k", k=16)
        s00 = p00[:].rearrange("q (g k) -> q g k", k=16)
        nc.scalar.copy(out=d10[:, :, 4:16], in_=s00[:, :, 0:12])
        nc.scalar.copy(out=d10[:, :, 0:4], in_=s00[:, :, 12:16])
        perms[(0, 0)] = p00
        perms[(1, 0)] = p10
        for rot in range(2):
            pr = keep.tile([P, P], F32, name="perm%d" % rot)
            d = pr[:].rearrange("q (g j) -> q g j", j=4)
            s = perms[(rot, 0)][:].rearrange("q (g j) -> q g j", j=4)
            nc.scalar.copy(out=d[:, :, 1:4], in_=s[:, :, 0:3])
            nc.scalar.copy(out=d[:, :, 0:1], in_=s[:, :, 3:4])
            perms[(rot, 1)] = pr

        nw = keep.tile([P, 4], F32)
        nb = keep.tile([P, 4], F32)
        nc.gpsimd.tensor_copy(out=nw[:], in_=nw_b[:])
        nc.gpsimd.tensor_copy(out=nb[:], in_=nb_b[:])

        spread = []
        for v in range(2):
            pv = psum.tile([P, C], F32)
            nc.tensor.matmul(pv[:], lhsT=ones[:], rhs=rows[:, v, :], start=True, stop=True)
            bc = keep.tile([P, C], BF16, name="bias%d" % v)
            nc.scalar.copy(out=bc[:], in_=pv[:])
            spread.append(bc)
        ob_bc, fb_bc = spread
        mints = {}
        st = {}

        def turn(cp, rp):
            if rp == 0:
                mint = three.tile([P, 4096], BF16, align_bytes=64)
                mints[cp] = mint
            mint = mints[cp]
            pt = psum.tile([P, 2, 2, P], F32)
            for k in range(2):
                r = 2 * rp + k
                src = (
                    obs[r // 4][:]
                    .rearrange("p s a d -> p (s a d)")
                    .bitcast(F32)
                )
                w0 = ((r % 4) * 8 + 2 * cp) * 128
                perm = perms[(1 if r >= 5 else 0, 1 if cp == 3 else 0)]
                for u in range(2):
                    nc.tensor.transpose(
                        pt[:, k, u, :], src[:, w0 + u : w0 + 256 : 2], perm[:]
                    )
            st[("pt", cp, rp)] = pt

        def turn_out(cp, rp):
            pt = st[("pt", cp, rp)]
            words = mints[cp][:].bitcast(F32).rearrange(
                "p (g h j u) -> p g h j u", h=8, j=4, u=2
            )
            for k in range(2):
                rho = (2 * rp + k + 3) % 8
                nc.scalar.copy(
                    out=words[:, :, rho, :, :],
                    in_=pt[:, k, :, :].rearrange("p u (g j) -> p g j u", j=4),
                )

        def add_bias(k):
            xb = xb_pool.tile([P, 2, C], F32)
            st[("xb", k)] = xb
            nc.vector.tensor_tensor(
                out=xb[:],
                in0=xts[divmod(k, 4)][:],
                in1=ob_bc[:].unsqueeze(1).to_broadcast([P, 2, C]),
                op=ALU.add,
            )

        def quantise_m(k):
            cp, b = divmod(k, 4)
            codes = three.tile([P, 256], U32, align_bytes=64)
            planes = three.tile([P, 256], U8, align_bytes=64)
            nc.vector.quantize_mx(
                out=codes[:].bitcast(FP8X4),
                scales=planes[:],
                in_=mints[cp][:, 1024 * b : 1024 * b + 1024],
            )
            st[("q1", k)] = (codes, planes)

        def first_matmul(k):
            codes, planes = st[("q1", k)]
            for c in range(2):
                py = psum.tile([P, C], F32)
                st[("py", k, c)] = py
                for warm_up in range(HEAT):
                    nc.tensor.matmul_mx(
                        out=py[:],
                        lhsT=codes[:, 0:128].bitcast(FP8X4),
                        lhsT_scale=planes[:, 0:128],
                        rhs=wz[:, 2 * c, :].bitcast(FP4X4),
                        rhs_scale=wzs[:, 2 * c, :],
                        start=True,
                        stop=True,
                    )
                for ah in range(2):
                    cols = slice(128 * ah, 128 * ah + 128)
                    nc.tensor.matmul_mx(
                        out=py[:],
                        lhsT=codes[:, cols].bitcast(FP8X4),
                        lhsT_scale=planes[:, cols],
                        rhs=wz[:, 2 * c + ah, :].bitcast(FP4X4),
                        rhs_scale=wzs[:, 2 * c + ah, :],
                        start=(ah == 0),
                        stop=(ah == 1),
                    )

        x2_tok = out_x2.rearrange("b (p e) c -> b p e c", e=8)
        x2_img = out_x2.rearrange("b (i j) c -> b i j c", j=H)
        g_tok = out_g.rearrange("b (p e) c -> b p e c", e=8)
        g_img = out_g.rearrange("b (i j) c -> b i j c", j=H)

        def store(k, tok, img, t):
            cp, b = divmod(k, 4)
            e = FIRST_E[cp]
            if cp == 2:
                nc.sync.dma_start(out=tok[b, :, e, :], in_=t[:, 0, :])
                for w in range(4):
                    nc.sync.dma_start(
                        out=img[b, :, 8 * ((w + 1) % 4), :], in_=t[w:P:4, 1, :]
                    )
            else:
                nc.sync.dma_start(out=tok[b, :, e : e + 2, :], in_=t[:])

        def residual(k, c):
            if c == 0:
                st[("x2", k)] = four.tile([P, 2, C], F32, name="x2")
                st[("sums", k)] = four.tile([P, 2], F32, name="sums")
                st[("ssq", k)] = four.tile([P, 2], F32, name="ssq")
            nc.vector.scalar_tensor_tensor(
                out=st[("x2", k)][:, c, :],
                in0=st[("py", k, c)][:],
                scalar=0.0,
                in1=st[("xb", k)][:, c, :],
                op0=ALU.add,
                op1=ALU.add,
                accum_out=st[("sums", k)][:, c : c + 1],
            )

        def squares(k, c):
            junk = two.tile([P, C], BF16)
            nc.scalar.activation(
                out=junk[:],
                in_=st[("x2", k)][:, c, :],
                func=ACT.Square,
                bias=st[("sums", k)][:, c : c + 1],
                scale=-512.0,
                accum_out=st[("ssq", k)][:, c : c + 1],
            )

        def statistics(k):
            nm = four.tile([P, 2], F32)
            var = four.tile([P, 2], F32)
            rstd = four.tile([P, 2], F32)
            nmr = four.tile([P, 2], F32)
            nc.gpsimd.tensor_scalar(
                out=nm[:],
                in0=st[("sums", k)][:],
                scalar1=-1.0 / 512,
                scalar2=0.0,
                op0=ALU.mult,
                op1=ALU.add,
            )
            nc.gpsimd.tensor_scalar(
                out=var[:],
                in0=st[("ssq", k)][:],
                scalar1=2.0**-27,
                scalar2=EPS,
                op0=ALU.mult,
                op1=ALU.add,
            )
            nc.gpsimd.tensor_tensor(out=rstd[:], in0=var[:], in1=half[:], op=ALU.pow)
            nc.gpsimd.tensor_tensor(out=nmr[:], in0=nm[:], in1=rstd[:], op=ALU.mult)
            st[("rstd", k)] = rstd
            st[("nmr", k)] = nmr
            store(k, x2_tok, x2_img, st[("x2", k)])

        def normalise(k, c):
            if c == 0:
                st[("z", k)] = two.tile([P, 2, C], F32, name="z")
            z = st[("z", k)]
            src = st[("x2", k)][:, c, :]
            rstd = st[("rstd", k)][:, c : c + 1]
            nmr = st[("nmr", k)][:, c : c + 1]
            if (2 * k + c) in ZDVE:
                nc.vector.tensor_scalar(
                    out=z[:, c, :],
                    in0=src,
                    scalar1=rstd,
                    scalar2=nmr,
                    op0=ALU.mult,
                    op1=ALU.add,
                )
            else:
                nc.scalar.activation(
                    out=z[:, c, :], in_=src, func=ACT.Identity, bias=nmr, scale=rstd
                )

        def turn_z(k, th):
            z = st[("z", k)]
            pz = psum.tile([P, 2, 256], F32)
            st[("pz", k, th)] = pz
            for t in range(2):
                for c in range(2):
                    nc.tensor.transpose(
                        pz[:, t, 128 * c : 128 * c + 128], z[:, c, 2 * th + t : C : 4], ident[:]
                    )

        def affine(k, th):
            if th == 0:
                st[("hp", k)] = two.tile([P, 4, 256], BF16, name="hp")
            for t in range(2):
                j = 2 * th + t
                nc.scalar.activation(
                    out=st[("hp", k)][:, j, :],
                    in_=st[("pz", k, th)][:, t, :],
                    func=ACT.Identity,
                    bias=nb[:, j : j + 1],
                    scale=nw[:, j : j + 1],
                )

        def interleave(k):
            hi = two.tile([P, 256, 4], BF16, align_bytes=64)
            st[("hi", k)] = hi
            nc.vector.tensor_copy(out=hi[:], in_=st[("hp", k)][:].rearrange("p t n -> p n t"))

        def quantise_h(k):
            codes2 = three.tile([P, 256], U32, align_bytes=64)
            planes2 = three.tile([P, 256], U8, align_bytes=64)
            nc.vector.quantize_mx(
                out=codes2[:].bitcast(FP8X4),
                scales=planes2[:],
                in_=st[("hi", k)][:].rearrange("p n t -> p (n t)"),
            )
            st[("q2", k)] = (codes2, planes2)

        def second_matmul(k):
            codes2, planes2 = st[("q2", k)]
            for c in range(2):
                pv = psum.tile([P, C], F32)
                st[("pv", k, c)] = pv
                cols = slice(128 * c, 128 * c + 128)
                nc.tensor.matmul_mx(
                    out=pv[:],
                    lhsT=codes2[:, cols].bitcast(FP8X4),
                    lhsT_scale=planes2[:, cols],
                    rhs=wf[:].bitcast(FP4X4),
                    rhs_scale=wfs[:],
                    start=True,
                    stop=True,
                )

        def bias_g(k, c):
            if c == 0:
                st[("v", k)] = two.tile([P, 2, C], F32, name="v")
            nc.vector.tensor_tensor(
                out=st[("v", k)][:, c, :], in0=st[("pv", k, c)][:], in1=fb_bc[:], op=ALU.add
            )

        def gelu(k):
            g = three.tile([P, 2, C], F32)
            if k < 15:
                nc.scalar.activation(out=g[:], in_=st[("v", k)][:], func=ACT.Gelu)
                store(k, g_tok, g_img, g)
            else:
                for c in range(2):
                    nc.scalar.activation(
                        out=g[:, c, :], in_=st[("v", k)][:, c, :], func=ACT.Gelu
                    )
                    nc.sync.dma_start(
                        out=g_tok[3, :, FIRST_E[3] + c, :], in_=g[:, c, :]
                    )

        ctx.enter_context(tc.manual_schedule())
        actions = {
            "X": lambda k: load_x(k // 4, k % 4) if k >= 4 else None,
            "B": add_bias,
            "Q": quantise_m,
            "M": first_matmul,
            "A0": lambda k: residual(k, 0),
            "A1": lambda k: residual(k, 1),
            "S0": lambda k: squares(k, 0),
            "S1": lambda k: squares(k, 1),
            "V": statistics,
            "N0": lambda k: normalise(k, 0),
            "N1": lambda k: normalise(k, 1),
            "T0": lambda k: turn_z(k, 0),
            "T1": lambda k: turn_z(k, 1),
            "E0": lambda k: affine(k, 0),
            "E1": lambda k: affine(k, 1),
            "I": interleave,
            "H": quantise_h,
            "K": second_matmul,
            "G0": lambda k: bias_g(k, 0),
            "G1": lambda k: bias_g(k, 1),
            "U": gelu,
            "R": lambda k: turn(k // 4, k % 4),
            "C": lambda k: turn_out(k // 4, k % 4),
        }
        lead = max(-lag for action, lag in ORDER)
        trail = max(lag for action, lag in ORDER)
        for i in range(-lead, 16 + trail):
            for action, lag in ORDER:
                if 0 <= i - lag < 16:
                    actions[action](i - lag)
